import numpy as np
import ml_dtypes

BF16 = ml_dtypes.bfloat16


def bf(x):
    return np.asarray(x, np.float32).astype(BF16)


def f32(x):
    return np.asarray(x, np.float32)


def f64(x):
    return np.asarray(x).astype(np.float64)


def striped(idx):
    return np.tile(idx.reshape(-1, 16).T, (8, 1))


C, S, N = 512, 256, 64
EPS = 1e-5


def setup_inputs():
    emb = np.random.standard_normal((C, S)) * (0.5 + np.random.rand(1, S)) + 0.5 * np.random.standard_normal((1, S))
    w = 1.0 + 0.1 * np.random.standard_normal((C, 1))
    sc = 0.3 * np.random.standard_normal((C, 1))
    sh = 0.5 * np.random.standard_normal((C, 1))
    idx = np.random.permutation(np.tile(np.arange(S), 2))[:N]
    return {"emb": f32(emb), "w": f32(w), "sc": f32(sc), "sh": f32(sh), "offs": striped(idx)}


def reference(emb, w, sc, sh, offs):
    idx = offs[:16].T.reshape(-1)
    e = f64(emb)
    mu = e.mean(axis=0, keepdims=True)
    var = np.square(e - mu).mean(axis=0, keepdims=True)
    z = (e - mu) / np.sqrt(var + EPS)
    a = f64(w) * (1.0 + f64(sc))
    return z[:, idx] * a + f64(sh)

@@ -1,0 +1,81 @@
+import concourse.mybir as mybir
+from concourse.masks import make_identity
+
+F32 = mybir.dt.float32
+U16 = mybir.dt.uint16
+ALU = mybir.AluOpType
+ACT = mybir.ActivationFunctionType
+
+P = 128
+C, S, N = 512, 256, 64
+BLOCKS = C // P
+EPS = 1e-5
+
+
+def tile_dit_kernel(tc, emb, w, sc, sh, offs, out):
+    nc = tc.nc
+    emb_blocks = emb.rearrange("(b p) s -> b p s", p=P)
+    out_blocks = out.rearrange("(b p) n -> b p n", p=P)
+
+    with (
+        tc.tile_pool(name="held", bufs=1) as held,
+        tc.psum_pool(name="psum", bufs=1) as psum,
+    ):
+        x = [held.tile([P, S], F32, name=f"x{b}") for b in range(BLOCKS)]
+        for b in range(BLOCKS):
+            queue = nc.sync if b % 2 == 0 else nc.scalar
+            queue.dma_start(x[b][:], emb_blocks[b])
+        offsets = held.tile([P, N // 16], U16, name="offsets")
+        nc.sync.dma_start(offsets[:], offs)
+        rows = held.tile([3 * BLOCKS, P], F32, name="rows")
+        for k, vector in enumerate((w, sc, sh)):
+            queue = nc.scalar if k % 2 == 0 else nc.sync
+            queue.dma_start(rows[k * BLOCKS : (k + 1) * BLOCKS, :], vector.rearrange("(b p) o -> b (p o)", p=P))
+
+        averager = held.tile([P, P], F32, name="averager")
+        nc.vector.memset(averager[:], 1.0 / C)
+        eps = held.tile([P, 1], F32, name="eps")
+        nc.vector.memset(eps[:], EPS)
+        ident = held.tile([3 * BLOCKS, 3 * BLOCKS], F32, name="ident")
+        make_identity(nc, ident[:])
+
+        mean_ps = psum.tile([P, S], F32, name="mean_ps")
+        for b in range(BLOCKS):
+            nc.tensor.matmul(mean_ps[:], averager[:], x[b][:], start=(b == 0), stop=(b == BLOCKS - 1))
+
+        cols_ps = psum.tile([P, 3 * BLOCKS], F32, name="cols_ps")
+        nc.tensor.matmul(cols_ps[:], rows[:], ident[:], start=True, stop=True)
+        cols = held.tile([P, 3 * BLOCKS], F32, name="cols")
+        nc.vector.tensor_copy(cols[:], cols_ps[:])
+        gain = cols[:, 0:BLOCKS]
+        scale = cols[:, BLOCKS : 2 * BLOCKS]
+        shift = cols[:, 2 * BLOCKS : 3 * BLOCKS]
+        a_repeated = held.tile([P, BLOCKS, N], F32, name="a_repeated")
+        nc.vector.scalar_tensor_tensor(
+            a_repeated[:],
+            scale.unsqueeze(2).to_broadcast([P, BLOCKS, N]),
+            1.0,
+            gain.unsqueeze(2).to_broadcast([P, BLOCKS, N]),
+            ALU.add,
+            ALU.mult,
+        )
+
+        centred = [held.tile([P, S], F32, name=f"centred{b}") for b in range(BLOCKS)]
+        squared = [held.tile([P, S], F32, name=f"squared{b}") for b in range(BLOCKS)]
+        var_ps = psum.tile([P, S], F32, name="var_ps")
+        for b in range(BLOCKS):
+            nc.vector.tensor_tensor(centred[b][:], x[b][:], mean_ps[:], ALU.subtract)
+            nc.vector.tensor_tensor(squared[b][:], centred[b][:], centred[b][:], ALU.mult)
+            nc.tensor.matmul(var_ps[:], averager[:], squared[b][:], start=(b == 0), stop=(b == BLOCKS - 1))
+        rstd = held.tile([P, S], F32, name="rstd")
+        nc.scalar.activation(rstd[:], var_ps[:], ACT.Abs_reciprocal_sqrt, bias=eps[:])
+
+        z = [held.tile([P, S], F32, name=f"z{b}") for b in range(BLOCKS)]
+        product = held.tile([P, BLOCKS, N], F32, name="product")
+        result = held.tile([P, BLOCKS, N], F32, name="result")
+        for b in range(BLOCKS):
+            nc.vector.tensor_tensor(z[b][:], centred[b][:], rstd[:], ALU.mult)
+            nc.vector.tensor_tensor(product[:, b, :], z[b][:].indirect(offsets[:]), a_repeated[:, b, :], ALU.mult)
+            nc.scalar.activation(result[:, b, :], product[:, b, :], ACT.Identity, bias=shift[:, b : b + 1])
+            queue = nc.sync if b % 2 == 0 else nc.scalar
+            queue.dma_start(out_blocks[b], result[:, b, :])

@@ -9,6 +9,8 @@ ACT = mybir.ActivationFunctionType
 P = 128
 C, S, N = 512, 256, 64
 BLOCKS = C // P
+HALVES = S // P
+STATS = 6
 EPS = 1e-5
 
 
@@ -32,19 +34,21 @@ def tile_dit_kernel(tc, emb, w, sc, sh, offs, out):
             queue = nc.scalar if k % 2 == 0 else nc.sync
             queue.dma_start(rows[k * BLOCKS : (k + 1) * BLOCKS, :], vector.rearrange("(b p) o -> b (p o)", p=P))
 
-        averager = held.tile([P, P], F32, name="averager")
-        nc.vector.memset(averager[:], 1.0 / C)
+        ident = held.tile([P, P], F32, name="ident")
+        make_identity(nc, ident[:])
         eps = held.tile([P, 1], F32, name="eps")
         nc.vector.memset(eps[:], EPS)
-        ident = held.tile([3 * BLOCKS, 3 * BLOCKS], F32, name="ident")
-        make_identity(nc, ident[:])
 
-        mean_ps = psum.tile([P, S], F32, name="mean_ps")
+        xT_ps = [psum.tile([P, HALVES, P], F32, name=f"xT_ps{b}") for b in range(BLOCKS)]
+        stats = held.tile([P, HALVES, BLOCKS * STATS], F32, name="stats")
         for b in range(BLOCKS):
-            nc.tensor.matmul(mean_ps[:], averager[:], x[b][:], start=(b == 0), stop=(b == BLOCKS - 1))
+            for h in range(HALVES):
+                nc.tensor.transpose(xT_ps[b][:, h, :], x[b][:, h * P : (h + 1) * P], ident[:])
+            for h in range(HALVES):
+                nc.vector.bn_stats(stats[:, h, b * STATS : (b + 1) * STATS], xT_ps[b][:, h, :])
 
         cols_ps = psum.tile([P, 3 * BLOCKS], F32, name="cols_ps")
-        nc.tensor.matmul(cols_ps[:], rows[:], ident[:], start=True, stop=True)
+        nc.tensor.matmul(cols_ps[:], rows[:], ident[0 : 3 * BLOCKS, 0 : 3 * BLOCKS], start=True, stop=True)
         cols = held.tile([P, 3 * BLOCKS], F32, name="cols")
         nc.vector.tensor_copy(cols[:], cols_ps[:])
         gain = cols[:, 0:BLOCKS]
@@ -60,22 +64,28 @@ def tile_dit_kernel(tc, emb, w, sc, sh, offs, out):
             ALU.mult,
         )
 
-        centred = [held.tile([P, S], F32, name=f"centred{b}") for b in range(BLOCKS)]
-        squared = [held.tile([P, S], F32, name=f"squared{b}") for b in range(BLOCKS)]
-        var_ps = psum.tile([P, S], F32, name="var_ps")
-        for b in range(BLOCKS):
-            nc.vector.tensor_tensor(centred[b][:], x[b][:], mean_ps[:], ALU.subtract)
-            nc.vector.tensor_tensor(squared[b][:], centred[b][:], centred[b][:], ALU.mult)
-            nc.tensor.matmul(var_ps[:], averager[:], squared[b][:], start=(b == 0), stop=(b == BLOCKS - 1))
-        rstd = held.tile([P, S], F32, name="rstd")
-        nc.scalar.activation(rstd[:], var_ps[:], ACT.Abs_reciprocal_sqrt, bias=eps[:])
+        mean_var = held.tile([P, HALVES, 2], F32, name="mean_var")
+        for h in range(HALVES):
+            nc.vector.bn_aggr(mean_var[:, h, :], stats[:, h, :])
+        std = held.tile([P, HALVES], F32, name="std")
+        nc.scalar.activation(std[:], mean_var[:, :, 1], ACT.Sqrt, bias=eps[:])
+        rstd = held.tile([P, HALVES], F32, name="rstd")
+        nc.vector.reciprocal(rstd[:], std[:])
 
-        z = [held.tile([P, S], F32, name=f"z{b}") for b in range(BLOCKS)]
         product = held.tile([P, BLOCKS, N], F32, name="product")
         result = held.tile([P, BLOCKS, N], F32, name="result")
         for b in range(BLOCKS):
-            nc.vector.tensor_tensor(z[b][:], centred[b][:], rstd[:], ALU.mult)
-            nc.vector.tensor_tensor(product[:, b, :], z[b][:].indirect(offsets[:]), a_repeated[:, b, :], ALU.mult)
+            zT = held.tile([P, HALVES, P], F32, name=f"zT{b}")
+            for h in range(HALVES):
+                nc.vector.tensor_scalar(
+                    zT[:, h, :], xT_ps[b][:, h, :], mean_var[:, h, 0:1], rstd[:, h : h + 1], ALU.subtract, ALU.mult
+                )
+            z_ps = psum.tile([P, S], F32, name="z_ps", bufs=3)
+            for h in range(HALVES):
+                nc.tensor.transpose(z_ps[:, h * P : (h + 1) * P], zT[:, h, :], ident[:])
+            z = held.tile([P, S], F32, name=f"z{b}")
+            nc.scalar.copy(z[:], z_ps[:])
+            nc.vector.tensor_tensor(product[:, b, :], z[:].indirect(offsets[:]), a_repeated[:, b, :], ALU.mult)
             nc.scalar.activation(result[:, b, :], product[:, b, :], ACT.Identity, bias=shift[:, b : b + 1])
             queue = nc.sync if b % 2 == 0 else nc.scalar
             queue.dma_start(out_blocks[b], result[:, b, :])

@@ -21,7 +21,7 @@ def tile_dit_kernel(tc, emb, w, sc, sh, offs, out):
 
     with (
         tc.tile_pool(name="held", bufs=1) as held,
-        tc.psum_pool(name="psum", bufs=1) as psum,
+        tc.psum_pool(name="flipped", bufs=1) as flipped,
     ):
         x = [held.tile([P, S], F32, name=f"x{b}") for b in range(BLOCKS)]
         for b in range(BLOCKS):
@@ -39,53 +39,64 @@ def tile_dit_kernel(tc, emb, w, sc, sh, offs, out):
         eps = held.tile([P, 1], F32, name="eps")
         nc.vector.memset(eps[:], EPS)
 
-        xT_ps = [psum.tile([P, HALVES, P], F32, name=f"xT_ps{b}") for b in range(BLOCKS)]
+        xT_ps = [flipped.tile([P, HALVES, P], F32, name=f"xT_ps{b}") for b in range(BLOCKS)]
         stats = held.tile([P, HALVES, BLOCKS * STATS], F32, name="stats")
+        mean_var = held.tile([P, HALVES, 2], F32, name="mean_var")
         for b in range(BLOCKS):
             for h in range(HALVES):
                 nc.tensor.transpose(xT_ps[b][:, h, :], x[b][:, h * P : (h + 1) * P], ident[:])
             for h in range(HALVES):
                 nc.vector.bn_stats(stats[:, h, b * STATS : (b + 1) * STATS], xT_ps[b][:, h, :])
+                if b == BLOCKS - 1:
+                    nc.vector.bn_aggr(mean_var[:, h, :], stats[:, h, :])
 
-        cols_ps = psum.tile([P, 3 * BLOCKS], F32, name="cols_ps")
-        nc.tensor.matmul(cols_ps[:], rows[:], ident[0 : 3 * BLOCKS, 0 : 3 * BLOCKS], start=True, stop=True)
+        std = held.tile([P, HALVES], F32, name="std")
+        rstd = held.tile([P, HALVES], F32, name="rstd")
+        for h in range(HALVES):
+            nc.scalar.activation(std[:, h : h + 1], mean_var[:, h, 1:2], ACT.Sqrt, bias=eps[:])
+
         cols = held.tile([P, 3 * BLOCKS], F32, name="cols")
-        nc.vector.tensor_copy(cols[:], cols_ps[:])
+        with tc.psum_pool(name="spread", bufs=1) as spread:
+            cols_ps = spread.tile([P, 3 * BLOCKS], F32, name="cols_ps")
+            nc.tensor.matmul(cols_ps[:], rows[:], ident[0 : 3 * BLOCKS, 0 : 3 * BLOCKS], start=True, stop=True)
+            nc.vector.tensor_copy(cols[:], cols_ps[:])
         gain = cols[:, 0:BLOCKS]
         scale = cols[:, BLOCKS : 2 * BLOCKS]
         shift = cols[:, 2 * BLOCKS : 3 * BLOCKS]
+        scale_plus_1 = held.tile([P, BLOCKS], F32, name="scale_plus_1")
+        nc.gpsimd.tensor_scalar(scale_plus_1[:], scale, 1.0, None, ALU.add)
         a_repeated = held.tile([P, BLOCKS, N], F32, name="a_repeated")
-        nc.vector.scalar_tensor_tensor(
+        nc.gpsimd.tensor_tensor(
             a_repeated[:],
-            scale.unsqueeze(2).to_broadcast([P, BLOCKS, N]),
-            1.0,
+            scale_plus_1[:].unsqueeze(2).to_broadcast([P, BLOCKS, N]),
             gain.unsqueeze(2).to_broadcast([P, BLOCKS, N]),
-            ALU.add,
             ALU.mult,
         )
 
-        mean_var = held.tile([P, HALVES, 2], F32, name="mean_var")
-        for h in range(HALVES):
-            nc.vector.bn_aggr(mean_var[:, h, :], stats[:, h, :])
-        std = held.tile([P, HALVES], F32, name="std")
-        nc.scalar.activation(std[:], mean_var[:, :, 1], ACT.Sqrt, bias=eps[:])
-        rstd = held.tile([P, HALVES], F32, name="rstd")
-        nc.vector.reciprocal(rstd[:], std[:])
+        with tc.psum_pool(name="back", bufs=1) as back:
+            zT = [held.tile([P, C], F32, name=f"zT{h}") for h in range(HALVES)]
+            z_ps = [back.tile([P, S], F32, name=f"z_ps{b}") for b in range(BLOCKS)]
+            z = [held.tile([P, S], F32, name=f"z{b}") for b in range(BLOCKS)]
+            for h in range(HALVES):
+                words = slice(h * P, (h + 1) * P)
+                nc.vector.reciprocal(rstd[:, h : h + 1], std[:, h : h + 1])
+                for b in range(BLOCKS):
+                    channels = slice(b * P, (b + 1) * P)
+                    nc.vector.tensor_scalar(
+                        zT[h][:, channels],
+                        xT_ps[b][:, h, :],
+                        mean_var[:, h, 0:1],
+                        rstd[:, h : h + 1],
+                        ALU.subtract,
+                        ALU.mult,
+                    )
+                    nc.tensor.transpose(z_ps[b][:, words], zT[h][:, channels], ident[:])
+                    nc.scalar.copy(z[b][:, words], z_ps[b][:, words])
 
-        product = held.tile([P, BLOCKS, N], F32, name="product")
-        result = held.tile([P, BLOCKS, N], F32, name="result")
-        for b in range(BLOCKS):
-            zT = held.tile([P, HALVES, P], F32, name=f"zT{b}")
-            for h in range(HALVES):
-                nc.vector.tensor_scalar(
-                    zT[:, h, :], xT_ps[b][:, h, :], mean_var[:, h, 0:1], rstd[:, h : h + 1], ALU.subtract, ALU.mult
-                )
-            z_ps = psum.tile([P, S], F32, name="z_ps", bufs=3)
-            for h in range(HALVES):
-                nc.tensor.transpose(z_ps[:, h * P : (h + 1) * P], zT[:, h, :], ident[:])
-            z = held.tile([P, S], F32, name=f"z{b}")
-            nc.scalar.copy(z[:], z_ps[:])
-            nc.vector.tensor_tensor(product[:, b, :], z[:].indirect(offsets[:]), a_repeated[:, b, :], ALU.mult)
-            nc.scalar.activation(result[:, b, :], product[:, b, :], ACT.Identity, bias=shift[:, b : b + 1])
-            queue = nc.sync if b % 2 == 0 else nc.scalar
-            queue.dma_start(out_blocks[b], result[:, b, :])
+            product = held.tile([P, BLOCKS, N], F32, name="product")
+            result = held.tile([P, BLOCKS, N], F32, name="result")
+            for b in range(BLOCKS):
+                nc.vector.tensor_tensor(product[:, b, :], z[b][:].indirect(offsets[:]), a_repeated[:, b, :], ALU.mult)
+                nc.scalar.activation(result[:, b, :], product[:, b, :], ACT.Identity, bias=shift[:, b : b + 1])
+                queue = nc.sync if b % 2 == 0 else nc.scalar
+                queue.dma_start(out_blocks[b], result[:, b, :])

@@ -42,17 +42,13 @@ def tile_dit_kernel(tc, emb, w, sc, sh, offs, out):
         xT_ps = [flipped.tile([P, HALVES, P], F32, name=f"xT_ps{b}") for b in range(BLOCKS)]
         stats = held.tile([P, HALVES, BLOCKS * STATS], F32, name="stats")
         mean_var = held.tile([P, HALVES, 2], F32, name="mean_var")
-        for b in range(BLOCKS):
-            for h in range(HALVES):
-                nc.tensor.transpose(xT_ps[b][:, h, :], x[b][:, h * P : (h + 1) * P], ident[:])
-            for h in range(HALVES):
-                nc.vector.bn_stats(stats[:, h, b * STATS : (b + 1) * STATS], xT_ps[b][:, h, :])
-                if b == BLOCKS - 1:
-                    nc.vector.bn_aggr(mean_var[:, h, :], stats[:, h, :])
-
         std = held.tile([P, HALVES], F32, name="std")
         rstd = held.tile([P, HALVES], F32, name="rstd")
         for h in range(HALVES):
+            for b in range(BLOCKS):
+                nc.tensor.transpose(xT_ps[b][:, h, :], x[b][:, h * P : (h + 1) * P], ident[:])
+                nc.vector.bn_stats(stats[:, h, b * STATS : (b + 1) * STATS], xT_ps[b][:, h, :])
+            nc.vector.bn_aggr(mean_var[:, h, :], stats[:, h, :])
             nc.scalar.activation(std[:, h : h + 1], mean_var[:, h, 1:2], ACT.Sqrt, bias=eps[:])
 
         cols = held.tile([P, 3 * BLOCKS], F32, name="cols")

@@ -21,7 +21,7 @@ def tile_dit_kernel(tc, emb, w, sc, sh, offs, out):
 
     with (
         tc.tile_pool(name="held", bufs=1) as held,
-        tc.psum_pool(name="flipped", bufs=1) as flipped,
+        tc.psum_pool(name="psum", bufs=1) as psum,
     ):
         x = [held.tile([P, S], F32, name=f"x{b}") for b in range(BLOCKS)]
         for b in range(BLOCKS):
@@ -39,60 +39,51 @@ def tile_dit_kernel(tc, emb, w, sc, sh, offs, out):
         eps = held.tile([P, 1], F32, name="eps")
         nc.vector.memset(eps[:], EPS)
 
-        xT_ps = [flipped.tile([P, HALVES, P], F32, name=f"xT_ps{b}") for b in range(BLOCKS)]
+        xT_ps = [psum.tile([P, HALVES, P], F32, name=f"xT_ps{b}") for b in range(BLOCKS)]
         stats = held.tile([P, HALVES, BLOCKS * STATS], F32, name="stats")
-        mean_var = held.tile([P, HALVES, 2], F32, name="mean_var")
-        std = held.tile([P, HALVES], F32, name="std")
-        rstd = held.tile([P, HALVES], F32, name="rstd")
-        for h in range(HALVES):
-            for b in range(BLOCKS):
+        for b in range(BLOCKS):
+            for h in range(HALVES):
                 nc.tensor.transpose(xT_ps[b][:, h, :], x[b][:, h * P : (h + 1) * P], ident[:])
+            for h in range(HALVES):
                 nc.vector.bn_stats(stats[:, h, b * STATS : (b + 1) * STATS], xT_ps[b][:, h, :])
-            nc.vector.bn_aggr(mean_var[:, h, :], stats[:, h, :])
-            nc.scalar.activation(std[:, h : h + 1], mean_var[:, h, 1:2], ACT.Sqrt, bias=eps[:])
 
+        cols_ps = psum.tile([P, 3 * BLOCKS], F32, name="cols_ps")
+        nc.tensor.matmul(cols_ps[:], rows[:], ident[0 : 3 * BLOCKS, 0 : 3 * BLOCKS], start=True, stop=True)
         cols = held.tile([P, 3 * BLOCKS], F32, name="cols")
-        with tc.psum_pool(name="spread", bufs=1) as spread:
-            cols_ps = spread.tile([P, 3 * BLOCKS], F32, name="cols_ps")
-            nc.tensor.matmul(cols_ps[:], rows[:], ident[0 : 3 * BLOCKS, 0 : 3 * BLOCKS], start=True, stop=True)
-            nc.vector.tensor_copy(cols[:], cols_ps[:])
+        nc.vector.tensor_copy(cols[:], cols_ps[:])
         gain = cols[:, 0:BLOCKS]
         scale = cols[:, BLOCKS : 2 * BLOCKS]
         shift = cols[:, 2 * BLOCKS : 3 * BLOCKS]
-        scale_plus_1 = held.tile([P, BLOCKS], F32, name="scale_plus_1")
-        nc.gpsimd.tensor_scalar(scale_plus_1[:], scale, 1.0, None, ALU.add)
         a_repeated = held.tile([P, BLOCKS, N], F32, name="a_repeated")
-        nc.gpsimd.tensor_tensor(
+        nc.vector.scalar_tensor_tensor(
             a_repeated[:],
-            scale_plus_1[:].unsqueeze(2).to_broadcast([P, BLOCKS, N]),
+            scale.unsqueeze(2).to_broadcast([P, BLOCKS, N]),
+            1.0,
             gain.unsqueeze(2).to_broadcast([P, BLOCKS, N]),
+            ALU.add,
             ALU.mult,
         )
 
-        with tc.psum_pool(name="back", bufs=1) as back:
-            zT = [held.tile([P, C], F32, name=f"zT{h}") for h in range(HALVES)]
-            z_ps = [back.tile([P, S], F32, name=f"z_ps{b}") for b in range(BLOCKS)]
-            z = [held.tile([P, S], F32, name=f"z{b}") for b in range(BLOCKS)]
-            for h in range(HALVES):
-                words = slice(h * P, (h + 1) * P)
-                nc.vector.reciprocal(rstd[:, h : h + 1], std[:, h : h + 1])
-                for b in range(BLOCKS):
-                    channels = slice(b * P, (b + 1) * P)
-                    nc.vector.tensor_scalar(
-                        zT[h][:, channels],
-                        xT_ps[b][:, h, :],
-                        mean_var[:, h, 0:1],
-                        rstd[:, h : h + 1],
-                        ALU.subtract,
-                        ALU.mult,
-                    )
-                    nc.tensor.transpose(z_ps[b][:, words], zT[h][:, channels], ident[:])
-                    nc.scalar.copy(z[b][:, words], z_ps[b][:, words])
+        mean_var = held.tile([P, HALVES, 2], F32, name="mean_var")
+        for h in range(HALVES):
+            nc.vector.bn_aggr(mean_var[:, h, :], stats[:, h, :])
+        rstd = held.tile([P, HALVES], F32, name="rstd")
+        nc.scalar.activation(rstd[:], mean_var[:, :, 1], ACT.Abs_reciprocal_sqrt, bias=eps[:])
 
-            product = held.tile([P, BLOCKS, N], F32, name="product")
-            result = held.tile([P, BLOCKS, N], F32, name="result")
-            for b in range(BLOCKS):
-                nc.vector.tensor_tensor(product[:, b, :], z[b][:].indirect(offsets[:]), a_repeated[:, b, :], ALU.mult)
-                nc.scalar.activation(result[:, b, :], product[:, b, :], ACT.Identity, bias=shift[:, b : b + 1])
-                queue = nc.sync if b % 2 == 0 else nc.scalar
-                queue.dma_start(out_blocks[b], result[:, b, :])
+        product = held.tile([P, BLOCKS, N], F32, name="product")
+        result = held.tile([P, BLOCKS, N], F32, name="result")
+        for b in range(BLOCKS):
+            zT = held.tile([P, HALVES, P], F32, name=f"zT{b}")
+            for h in range(HALVES):
+                nc.vector.tensor_scalar(
+                    zT[:, h, :], xT_ps[b][:, h, :], mean_var[:, h, 0:1], rstd[:, h : h + 1], ALU.subtract, ALU.mult
+                )
+            z_ps = psum.tile([P, S], F32, name="z_ps", bufs=3)
+            for h in range(HALVES):
+                nc.tensor.transpose(z_ps[:, h * P : (h + 1) * P], zT[:, h, :], ident[:])
+            z = held.tile([P, S], F32, name=f"z{b}")
+            nc.scalar.copy(z[:], z_ps[:])
+            nc.vector.tensor_tensor(product[:, b, :], z[:].indirect(offsets[:]), a_repeated[:, b, :], ALU.mult)
+            nc.scalar.activation(result[:, b, :], product[:, b, :], ACT.Identity, bias=shift[:, b : b + 1])
+            queue = nc.sync if b % 2 == 0 else nc.scalar
+            queue.dma_start(out_blocks[b], result[:, b, :])

@@ -25,14 +25,12 @@ def tile_dit_kernel(tc, emb, w, sc, sh, offs, out):
     ):
         x = [held.tile([P, S], F32, name=f"x{b}") for b in range(BLOCKS)]
         for b in range(BLOCKS):
-            queue = nc.sync if b % 2 == 0 else nc.scalar
-            queue.dma_start(x[b][:], emb_blocks[b])
+            nc.sync.dma_start(x[b][:], emb_blocks[b])
         offsets = held.tile([P, N // 16], U16, name="offsets")
         nc.sync.dma_start(offsets[:], offs)
         rows = held.tile([3 * BLOCKS, P], F32, name="rows")
         for k, vector in enumerate((w, sc, sh)):
-            queue = nc.scalar if k % 2 == 0 else nc.sync
-            queue.dma_start(rows[k * BLOCKS : (k + 1) * BLOCKS, :], vector.rearrange("(b p) o -> b (p o)", p=P))
+            nc.scalar.dma_start(rows[k * BLOCKS : (k + 1) * BLOCKS, :], vector.rearrange("(b p) o -> b (p o)", p=P))
 
         ident = held.tile([P, P], F32, name="ident")
         make_identity(nc, ident[:])

@@ -10,78 +10,81 @@ P = 128
 C, S, N = 512, 256, 64
 BLOCKS = C // P
 HALVES = S // P
+PAIRS = BLOCKS // 2
 STATS = 6
 EPS = 1e-5
 
 
 def tile_dit_kernel(tc, emb, w, sc, sh, offs, out):
     nc = tc.nc
-    emb_blocks = emb.rearrange("(b p) s -> b p s", p=P)
-    out_blocks = out.rearrange("(b p) n -> b p n", p=P)
+    emb_blocks = emb.rearrange("(p b) s -> p b s", b=BLOCKS)
+    out_blocks = out.rearrange("(p b) n -> p b n", b=BLOCKS)
 
     with (
         tc.tile_pool(name="held", bufs=1) as held,
         tc.psum_pool(name="psum", bufs=1) as psum,
     ):
-        x = [held.tile([P, S], F32, name=f"x{b}") for b in range(BLOCKS)]
-        for b in range(BLOCKS):
-            nc.sync.dma_start(x[b][:], emb_blocks[b])
+        x = [[held.tile([P, 2 * P], F32, name=f"x{h}{q}") for q in range(PAIRS)] for h in range(HALVES)]
+        for h in range(HALVES):
+            for q in range(PAIRS):
+                nc.sync.dma_start(
+                    x[h][q][:].rearrange("p (i s) -> p i s", i=2),
+                    emb_blocks[:, 2 * q : 2 * q + 2, h * P : (h + 1) * P],
+                )
         offsets = held.tile([P, N // 16], U16, name="offsets")
         nc.sync.dma_start(offsets[:], offs)
-        rows = held.tile([3 * BLOCKS, P], F32, name="rows")
-        for k, vector in enumerate((w, sc, sh)):
-            nc.scalar.dma_start(rows[k * BLOCKS : (k + 1) * BLOCKS, :], vector.rearrange("(b p) o -> b (p o)", p=P))
+        gain = held.tile([P, BLOCKS], F32, name="gain")
+        scale = held.tile([P, BLOCKS], F32, name="scale")
+        shift = held.tile([P, BLOCKS], F32, name="shift")
+        for tile, vector in ((gain, w), (scale, sc), (shift, sh)):
+            nc.scalar.dma_start(tile[:], vector.rearrange("(p b) o -> p (b o)", b=BLOCKS))
 
         ident = held.tile([P, P], F32, name="ident")
         make_identity(nc, ident[:])
         eps = held.tile([P, 1], F32, name="eps")
         nc.vector.memset(eps[:], EPS)
 
-        xT_ps = [psum.tile([P, HALVES, P], F32, name=f"xT_ps{b}") for b in range(BLOCKS)]
-        stats = held.tile([P, HALVES, BLOCKS * STATS], F32, name="stats")
-        for b in range(BLOCKS):
-            for h in range(HALVES):
-                nc.tensor.transpose(xT_ps[b][:, h, :], x[b][:, h * P : (h + 1) * P], ident[:])
-            for h in range(HALVES):
-                nc.vector.bn_stats(stats[:, h, b * STATS : (b + 1) * STATS], xT_ps[b][:, h, :])
-
-        cols_ps = psum.tile([P, 3 * BLOCKS], F32, name="cols_ps")
-        nc.tensor.matmul(cols_ps[:], rows[:], ident[0 : 3 * BLOCKS, 0 : 3 * BLOCKS], start=True, stop=True)
-        cols = held.tile([P, 3 * BLOCKS], F32, name="cols")
-        nc.vector.tensor_copy(cols[:], cols_ps[:])
-        gain = cols[:, 0:BLOCKS]
-        scale = cols[:, BLOCKS : 2 * BLOCKS]
-        shift = cols[:, 2 * BLOCKS : 3 * BLOCKS]
         a_repeated = held.tile([P, BLOCKS, N], F32, name="a_repeated")
         nc.vector.scalar_tensor_tensor(
             a_repeated[:],
-            scale.unsqueeze(2).to_broadcast([P, BLOCKS, N]),
+            scale[:].unsqueeze(2).to_broadcast([P, BLOCKS, N]),
             1.0,
-            gain.unsqueeze(2).to_broadcast([P, BLOCKS, N]),
+            gain[:].unsqueeze(2).to_broadcast([P, BLOCKS, N]),
             ALU.add,
             ALU.mult,
         )
 
+        xT_ps = [[psum.tile([P, 2 * P], F32, name=f"xT_ps{h}{q}") for q in range(PAIRS)] for h in range(HALVES)]
+        stats = held.tile([P, HALVES, PAIRS * STATS], F32, name="stats")
         mean_var = held.tile([P, HALVES, 2], F32, name="mean_var")
-        for h in range(HALVES):
-            nc.vector.bn_aggr(mean_var[:, h, :], stats[:, h, :])
         rstd = held.tile([P, HALVES], F32, name="rstd")
-        nc.scalar.activation(rstd[:], mean_var[:, :, 1], ACT.Abs_reciprocal_sqrt, bias=eps[:])
+        for h in range(HALVES):
+            for q in range(PAIRS):
+                for i in range(2):
+                    nc.tensor.transpose(xT_ps[h][q][:, i * P : (i + 1) * P], x[h][q][:, i * P : (i + 1) * P], ident[:])
+                nc.vector.bn_stats(stats[:, h, q * STATS : (q + 1) * STATS], xT_ps[h][q][:])
+            nc.vector.bn_aggr(mean_var[:, h, :], stats[:, h, :])
+            nc.scalar.activation(rstd[:, h : h + 1], mean_var[:, h, 1:2], ACT.Abs_reciprocal_sqrt, bias=eps[:])
+
+        z = [held.tile([P, S], F32, name=f"z{b}") for b in range(BLOCKS)]
+        for h in range(HALVES):
+            for q in range(PAIRS):
+                zT = held.tile([P, 2 * P], F32, name=f"zT{h}{q}")
+                z_ps = psum.tile([P, 2 * P], F32, name=f"z_ps{h}{q}")
+                for i in range(2):
+                    block = slice(i * P, (i + 1) * P)
+                    nc.vector.tensor_scalar(
+                        zT[:, block], xT_ps[h][q][:, block], mean_var[:, h, 0:1], rstd[:, h : h + 1], ALU.subtract, ALU.mult
+                    )
+                for i in range(2):
+                    block = slice(i * P, (i + 1) * P)
+                    nc.tensor.transpose(z_ps[:, block], zT[:, block], ident[:])
+                for i in range(2):
+                    nc.scalar.copy(z[2 * q + i][:, h * P : (h + 1) * P], z_ps[:, i * P : (i + 1) * P])
 
         product = held.tile([P, BLOCKS, N], F32, name="product")
         result = held.tile([P, BLOCKS, N], F32, name="result")
         for b in range(BLOCKS):
-            zT = held.tile([P, HALVES, P], F32, name=f"zT{b}")
-            for h in range(HALVES):
-                nc.vector.tensor_scalar(
-                    zT[:, h, :], xT_ps[b][:, h, :], mean_var[:, h, 0:1], rstd[:, h : h + 1], ALU.subtract, ALU.mult
-                )
-            z_ps = psum.tile([P, S], F32, name="z_ps", bufs=3)
-            for h in range(HALVES):
-                nc.tensor.transpose(z_ps[:, h * P : (h + 1) * P], zT[:, h, :], ident[:])
-            z = held.tile([P, S], F32, name=f"z{b}")
-            nc.scalar.copy(z[:], z_ps[:])
-            nc.vector.tensor_tensor(product[:, b, :], z[:].indirect(offsets[:]), a_repeated[:, b, :], ALU.mult)
-            nc.scalar.activation(result[:, b, :], product[:, b, :], ACT.Identity, bias=shift[:, b : b + 1])
-            queue = nc.sync if b % 2 == 0 else nc.scalar
-            queue.dma_start(out_blocks[b], result[:, b, :])
+            nc.vector.tensor_tensor(product[:, b, :], z[b][:].indirect(offsets[:]), a_repeated[:, b, :], ALU.mult)
+            nc.vector.tensor_scalar_add(result[:, b, :], product[:, b, :], shift[:, b : b + 1])
+            nc.sync.dma_start(out_blocks[:, b, :], result[:, b, :])

@@ -11,6 +11,7 @@ C, S, N = 512, 256, 64
 BLOCKS = C // P
 HALVES = S // P
 PAIRS = BLOCKS // 2
+BANKS = 8
 STATS = 6
 EPS = 1e-5
 
@@ -22,7 +23,7 @@ def tile_dit_kernel(tc, emb, w, sc, sh, offs, out):
 
     with (
         tc.tile_pool(name="held", bufs=1) as held,
-        tc.psum_pool(name="psum", bufs=1) as psum,
+        tc.psum_pool(name="psum", bufs=BANKS) as psum,
     ):
         x = [[held.tile([P, 2 * P], F32, name=f"x{h}{q}") for q in range(PAIRS)] for h in range(HALVES)]
         for h in range(HALVES):
@@ -54,37 +55,32 @@ def tile_dit_kernel(tc, emb, w, sc, sh, offs, out):
             ALU.mult,
         )
 
-        xT_ps = [[psum.tile([P, 2 * P], F32, name=f"xT_ps{h}{q}") for q in range(PAIRS)] for h in range(HALVES)]
-        stats = held.tile([P, HALVES, PAIRS * STATS], F32, name="stats")
+        xT_ps = [[psum.tile([P, P], F32, name=f"xT_ps{h}{b}", tag="bank") for b in range(BLOCKS)] for h in range(HALVES)]
+        stats = held.tile([P, HALVES, BLOCKS * STATS], F32, name="stats")
         mean_var = held.tile([P, HALVES, 2], F32, name="mean_var")
         rstd = held.tile([P, HALVES], F32, name="rstd")
         for h in range(HALVES):
-            for q in range(PAIRS):
-                for i in range(2):
-                    nc.tensor.transpose(xT_ps[h][q][:, i * P : (i + 1) * P], x[h][q][:, i * P : (i + 1) * P], ident[:])
-                nc.vector.bn_stats(stats[:, h, q * STATS : (q + 1) * STATS], xT_ps[h][q][:])
+            for b in range(BLOCKS):
+                q, i = divmod(b, 2)
+                nc.tensor.transpose(xT_ps[h][b][:], x[h][q][:, i * P : (i + 1) * P], ident[:])
+                nc.vector.bn_stats(stats[:, h, b * STATS : (b + 1) * STATS], xT_ps[h][b][:])
             nc.vector.bn_aggr(mean_var[:, h, :], stats[:, h, :])
             nc.scalar.activation(rstd[:, h : h + 1], mean_var[:, h, 1:2], ACT.Abs_reciprocal_sqrt, bias=eps[:])
 
         z = [held.tile([P, S], F32, name=f"z{b}") for b in range(BLOCKS)]
         for h in range(HALVES):
-            for q in range(PAIRS):
-                zT = held.tile([P, 2 * P], F32, name=f"zT{h}{q}")
-                z_ps = psum.tile([P, 2 * P], F32, name=f"z_ps{h}{q}")
-                for i in range(2):
-                    block = slice(i * P, (i + 1) * P)
-                    nc.vector.tensor_scalar(
-                        zT[:, block], xT_ps[h][q][:, block], mean_var[:, h, 0:1], rstd[:, h : h + 1], ALU.subtract, ALU.mult
-                    )
-                for i in range(2):
-                    block = slice(i * P, (i + 1) * P)
-                    nc.tensor.transpose(z_ps[:, block], zT[:, block], ident[:])
-                for i in range(2):
-                    nc.scalar.copy(z[2 * q + i][:, h * P : (h + 1) * P], z_ps[:, i * P : (i + 1) * P])
+            for b in range(BLOCKS):
+                zT = held.tile([P, P], F32, name=f"zT{h}{b}")
+                nc.vector.tensor_scalar(
+                    zT[:], xT_ps[h][b][:], mean_var[:, h, 0:1], rstd[:, h : h + 1], ALU.subtract, ALU.mult
+                )
+                z_ps = psum.tile([P, P], F32, name=f"z_ps{h}{b}", tag="bank")
+                nc.tensor.transpose(z_ps[:], zT[:], ident[:])
+                nc.scalar.copy(z[b][:, h * P : (h + 1) * P], z_ps[:])
 
         product = held.tile([P, BLOCKS, N], F32, name="product")
         result = held.tile([P, BLOCKS, N], F32, name="result")
         for b in range(BLOCKS):
             nc.vector.tensor_tensor(product[:, b, :], z[b][:].indirect(offsets[:]), a_repeated[:, b, :], ALU.mult)
-            nc.vector.tensor_scalar_add(result[:, b, :], product[:, b, :], shift[:, b : b + 1])
+            nc.scalar.activation(result[:, b, :], product[:, b, :], ACT.Identity, bias=shift[:, b : b + 1])
             nc.sync.dma_start(out_blocks[:, b, :], result[:, b, :])

@@ -82,5 +82,8 @@ def tile_dit_kernel(tc, emb, w, sc, sh, offs, out):
         result = held.tile([P, BLOCKS, N], F32, name="result")
         for b in range(BLOCKS):
             nc.vector.tensor_tensor(product[:, b, :], z[b][:].indirect(offsets[:]), a_repeated[:, b, :], ALU.mult)
-            nc.scalar.activation(result[:, b, :], product[:, b, :], ACT.Identity, bias=shift[:, b : b + 1])
+            if b < BLOCKS - 1:
+                nc.scalar.activation(result[:, b, :], product[:, b, :], ACT.Identity, bias=shift[:, b : b + 1])
+            else:
+                nc.vector.tensor_scalar_add(result[:, b, :], product[:, b, :], shift[:, b : b + 1])
             nc.sync.dma_start(out_blocks[:, b, :], result[:, b, :])

@@ -38,22 +38,12 @@ def tile_dit_kernel(tc, emb, w, sc, sh, offs, out):
         scale = held.tile([P, BLOCKS], F32, name="scale")
         shift = held.tile([P, BLOCKS], F32, name="shift")
         for tile, vector in ((gain, w), (scale, sc), (shift, sh)):
-            nc.scalar.dma_start(tile[:], vector.rearrange("(p b) o -> p (b o)", b=BLOCKS))
+            nc.sync.dma_start(tile[:], vector.rearrange("(p b) o -> p (b o)", b=BLOCKS))
 
         ident = held.tile([P, P], F32, name="ident")
         make_identity(nc, ident[:])
         eps = held.tile([P, 1], F32, name="eps")
         nc.vector.memset(eps[:], EPS)
-
-        a_repeated = held.tile([P, BLOCKS, N], F32, name="a_repeated")
-        nc.vector.scalar_tensor_tensor(
-            a_repeated[:],
-            scale[:].unsqueeze(2).to_broadcast([P, BLOCKS, N]),
-            1.0,
-            gain[:].unsqueeze(2).to_broadcast([P, BLOCKS, N]),
-            ALU.add,
-            ALU.mult,
-        )
 
         xT_ps = [[psum.tile([P, P], F32, name=f"xT_ps{h}{b}", tag="bank") for b in range(BLOCKS)] for h in range(HALVES)]
         stats = held.tile([P, HALVES, BLOCKS * STATS], F32, name="stats")
@@ -77,6 +67,16 @@ def tile_dit_kernel(tc, emb, w, sc, sh, offs, out):
                 z_ps = psum.tile([P, P], F32, name=f"z_ps{h}{b}", tag="bank")
                 nc.tensor.transpose(z_ps[:], zT[:], ident[:])
                 nc.scalar.copy(z[b][:, h * P : (h + 1) * P], z_ps[:])
+
+        scale_plus_1 = held.tile([P, BLOCKS], F32, name="scale_plus_1")
+        nc.gpsimd.tensor_scalar_add(scale_plus_1[:], scale[:], 1.0)
+        a_repeated = held.tile([P, BLOCKS, N], F32, name="a_repeated")
+        nc.gpsimd.tensor_tensor(
+            a_repeated[:],
+            scale_plus_1[:].unsqueeze(2).to_broadcast([P, BLOCKS, N]),
+            gain[:].unsqueeze(2).to_broadcast([P, BLOCKS, N]),
+            ALU.mult,
+        )
 
         product = held.tile([P, BLOCKS, N], F32, name="product")
         result = held.tile([P, BLOCKS, N], F32, name="result")

@@ -10,7 +10,6 @@ P = 128
 C, S, N = 512, 256, 64
 BLOCKS = C // P
 HALVES = S // P
-PAIRS = BLOCKS // 2
 BANKS = 8
 STATS = 6
 EPS = 1e-5
@@ -25,13 +24,10 @@ def tile_dit_kernel(tc, emb, w, sc, sh, offs, out):
         tc.tile_pool(name="held", bufs=1) as held,
         tc.psum_pool(name="psum", bufs=BANKS) as psum,
     ):
-        x = [[held.tile([P, 2 * P], F32, name=f"x{h}{q}") for q in range(PAIRS)] for h in range(HALVES)]
+        x = [[held.tile([P, P], F32, name=f"x{h}{b}") for b in range(BLOCKS)] for h in range(HALVES)]
         for h in range(HALVES):
-            for q in range(PAIRS):
-                nc.sync.dma_start(
-                    x[h][q][:].rearrange("p (i s) -> p i s", i=2),
-                    emb_blocks[:, 2 * q : 2 * q + 2, h * P : (h + 1) * P],
-                )
+            for b in range(BLOCKS):
+                nc.sync.dma_start(x[h][b][:], emb_blocks[:, b, h * P : (h + 1) * P])
         offsets = held.tile([P, N // 16], U16, name="offsets")
         nc.sync.dma_start(offsets[:], offs)
         gain = held.tile([P, BLOCKS], F32, name="gain")
@@ -51,8 +47,7 @@ def tile_dit_kernel(tc, emb, w, sc, sh, offs, out):
         rstd = held.tile([P, HALVES], F32, name="rstd")
         for h in range(HALVES):
             for b in range(BLOCKS):
-                q, i = divmod(b, 2)
-                nc.tensor.transpose(xT_ps[h][b][:], x[h][q][:, i * P : (i + 1) * P], ident[:])
+                nc.tensor.transpose(xT_ps[h][b][:], x[h][b][:], ident[:])
                 nc.vector.bn_stats(stats[:, h, b * STATS : (b + 1) * STATS], xT_ps[h][b][:])
             nc.vector.bn_aggr(mean_var[:, h, :], stats[:, h, :])
             nc.scalar.activation(rstd[:, h : h + 1], mean_var[:, h, 1:2], ACT.Abs_reciprocal_sqrt, bias=eps[:])

@@ -17,8 +17,8 @@ EPS = 1e-5
 
 def tile_dit_kernel(tc, emb, w, sc, sh, offs, out):
     nc = tc.nc
-    emb_blocks = emb.rearrange("(p b) s -> p b s", b=BLOCKS)
-    out_blocks = out.rearrange("(p b) n -> p b n", b=BLOCKS)
+    emb_blocks = emb.rearrange("(b p) s -> p b s", p=P)
+    out_blocks = out.rearrange("(b p) n -> p b n", p=P)
 
     with (
         tc.tile_pool(name="held", bufs=1) as held,
@@ -34,7 +34,7 @@ def tile_dit_kernel(tc, emb, w, sc, sh, offs, out):
         scale = held.tile([P, BLOCKS], F32, name="scale")
         shift = held.tile([P, BLOCKS], F32, name="shift")
         for tile, vector in ((gain, w), (scale, sc), (shift, sh)):
-            nc.sync.dma_start(tile[:], vector.rearrange("(p b) o -> p (b o)", b=BLOCKS))
+            nc.sync.dma_start(tile[:], vector.rearrange("(b p) o -> p (b o)", p=P))
 
         ident = held.tile([P, P], F32, name="ident")
         make_identity(nc, ident[:])

import concourse.mybir as mybir
from concourse.masks import make_identity

F32 = mybir.dt.float32
U16 = mybir.dt.uint16
ALU = mybir.AluOpType
ACT = mybir.ActivationFunctionType

P = 128
C, S, N = 512, 256, 64
BLOCKS = C // P
HALVES = S // P
BANKS = 8
STATS = 6
EPS = 1e-5


def tile_dit_kernel(tc, emb, w, sc, sh, offs, out):
    nc = tc.nc
    emb_blocks = emb.rearrange("(b p) s -> p b s", p=P)
    out_blocks = out.rearrange("(b p) n -> p b n", p=P)

    with (
        tc.tile_pool(name="held", bufs=1) as held,
        tc.psum_pool(name="psum", bufs=BANKS) as psum,
    ):
        x = [[held.tile([P, P], F32, name=f"x{h}{b}") for b in range(BLOCKS)] for h in range(HALVES)]
        for h in range(HALVES):
            for b in range(BLOCKS):
                nc.sync.dma_start(x[h][b][:], emb_blocks[:, b, h * P : (h + 1) * P])
        offsets = held.tile([P, N // 16], U16, name="offsets")
        nc.sync.dma_start(offsets[:], offs)
        gain = held.tile([P, BLOCKS], F32, name="gain")
        scale = held.tile([P, BLOCKS], F32, name="scale")
        shift = held.tile([P, BLOCKS], F32, name="shift")
        for tile, vector in ((gain, w), (scale, sc), (shift, sh)):
            nc.sync.dma_start(tile[:], vector.rearrange("(b p) o -> p (b o)", p=P))

        ident = held.tile([P, P], F32, name="ident")
        make_identity(nc, ident[:])
        eps = held.tile([P, 1], F32, name="eps")
        nc.vector.memset(eps[:], EPS)

        xT_ps = [[psum.tile([P, P], F32, name=f"xT_ps{h}{b}", tag="bank") for b in range(BLOCKS)] for h in range(HALVES)]
        stats = held.tile([P, HALVES, BLOCKS * STATS], F32, name="stats")
        mean_var = held.tile([P, HALVES, 2], F32, name="mean_var")
        rstd = held.tile([P, HALVES], F32, name="rstd")
        for h in range(HALVES):
            for b in range(BLOCKS):
                nc.tensor.transpose(xT_ps[h][b][:], x[h][b][:], ident[:])
                nc.vector.bn_stats(stats[:, h, b * STATS : (b + 1) * STATS], xT_ps[h][b][:])
            nc.vector.bn_aggr(mean_var[:, h, :], stats[:, h, :])
            nc.scalar.activation(rstd[:, h : h + 1], mean_var[:, h, 1:2], ACT.Abs_reciprocal_sqrt, bias=eps[:])

        z = [held.tile([P, S], F32, name=f"z{b}") for b in range(BLOCKS)]
        for h in range(HALVES):
            for b in range(BLOCKS):
                zT = held.tile([P, P], F32, name=f"zT{h}{b}")
                nc.vector.tensor_scalar(
                    zT[:], xT_ps[h][b][:], mean_var[:, h, 0:1], rstd[:, h : h + 1], ALU.subtract, ALU.mult
                )
                z_ps = psum.tile([P, P], F32, name=f"z_ps{h}{b}", tag="bank")
                nc.tensor.transpose(z_ps[:], zT[:], ident[:])
                nc.scalar.copy(z[b][:, h * P : (h + 1) * P], z_ps[:])

        scale_plus_1 = held.tile([P, BLOCKS], F32, name="scale_plus_1")
        nc.gpsimd.tensor_scalar_add(scale_plus_1[:], scale[:], 1.0)
        a_repeated = held.tile([P, BLOCKS, N], F32, name="a_repeated")
        nc.gpsimd.tensor_tensor(
            a_repeated[:],
            scale_plus_1[:].unsqueeze(2).to_broadcast([P, BLOCKS, N]),
            gain[:].unsqueeze(2).to_broadcast([P, BLOCKS, N]),
            ALU.mult,
        )

        product = held.tile([P, BLOCKS, N], F32, name="product")
        result = held.tile([P, BLOCKS, N], F32, name="result")
        for b in range(BLOCKS):
            nc.vector.tensor_tensor(product[:, b, :], z[b][:].indirect(offsets[:]), a_repeated[:, b, :], ALU.mult)
            if b < BLOCKS - 1:
                nc.scalar.activation(result[:, b, :], product[:, b, :], ACT.Identity, bias=shift[:, b : b + 1])
            else:
                nc.vector.tensor_scalar_add(result[:, b, :], product[:, b, :], shift[:, b : b + 1])
            nc.sync.dma_start(out_blocks[:, b, :], result[:, b, :])
